import numpy as np
import ml_dtypes


def mxq(x, axis, fmt="e4m3"):
    dtype, down = {"e4m3": (ml_dtypes.float8_e4m3fn, 7), "e5m2": (ml_dtypes.float8_e5m2, 14)}[fmt]
    v = np.moveaxis(np.asarray(x, np.float32).astype(ml_dtypes.bfloat16).astype(np.float64), axis, -1)
    blocks = v.reshape(v.shape[:-1] + (-1, 32))
    amax = np.abs(blocks).max(-1, keepdims=True)
    byte = np.maximum(np.where(amax > 0, np.frexp(amax)[1] - 1 + 127, 0) - down, 1)
    scale = np.exp2(byte - 127.0)
    codes = (blocks / scale).astype(np.float32).astype(dtype).astype(np.float64)
    return np.moveaxis((codes * scale).reshape(v.shape), -1, axis)


WIDE = False


def mx_kscale(k):
    if not WIDE:
        return np.ones(k)
    levels = np.array([10, -10, 5, -5, 0])
    if k % 512:
        return np.exp2(np.random.permutation(np.resize(levels, k // 32))).repeat(32)
    a = np.empty((k // 512, 16))
    for p in range(k // 512):
        a[p, :8] = np.random.permutation(np.resize(levels, 8))
        for g in range(8):
            far = levels[np.abs(levels - a[p, g]) >= 10]
            a[p, g + 8] = far[np.random.randint(len(far))]
    return np.exp2(a.ravel()).repeat(32)


BF16 = ml_dtypes.bfloat16


def bf(x):
    return np.asarray(x, np.float32).astype(BF16)


def f64(x):
    return np.asarray(x).astype(np.float64)


E2M1 = np.array([0.0, 0.5, 1.0, 1.5, 2.0, 3.0, 4.0, 6.0, -0.0, -0.5, -1.0, -1.5, -2.0, -3.0, -4.0, -6.0])


def pack_weight(w, fmt):
    k, n = w.shape
    w = f64(bf(w)).reshape(k // 32, 32, n)
    amax = np.abs(w).max(1)
    if fmt == "e4m3":
        byte = np.frexp(amax)[1] - 1 + 127 - 7
    else:
        mant, ex = np.frexp(amax / 6.0)
        byte = np.where(mant > 0.5, ex, ex - 1) + 127
    byte = np.clip(np.where(amax > 0, byte, 1), 1, 254)
    scaled = (w * np.exp2(127.0 - byte)[:, None, :]).reshape(k, n).astype(np.float32)
    by_word = np.ascontiguousarray(scaled.reshape(k // 512, 128, 4, n).transpose(0, 1, 3, 2))
    if fmt == "e4m3":
        words = by_word.astype(ml_dtypes.float8_e4m3fn).view(np.uint8)
    else:
        c = by_word.astype(ml_dtypes.float4_e2m1fn).view(np.uint8) & 0xF
        words = c[..., 0::2] | (c[..., 1::2] << 4)
    return np.ascontiguousarray(words), np.ascontiguousarray(byte.astype(np.uint8).reshape(k // 512, 16, n))


def unpack_weight(words, scales, fmt):
    g, p, n, _ = words.shape
    if fmt == "e4m3":
        vals = np.ascontiguousarray(words).view(ml_dtypes.float8_e4m3fn).astype(np.float64)
    else:
        nib = np.empty((g, p, n, 4), np.uint8)
        nib[..., 0::2] = words & 0xF
        nib[..., 1::2] = words >> 4
        vals = E2M1[nib]
    vals = vals * np.repeat(np.exp2(scales.astype(np.float64) - 127.0), 8, axis=1)[..., None]
    return vals.transpose(0, 1, 3, 2).reshape(g * 512, n)
def pack4(w):
    words, scales = pack_weight(w, "e2m1")
    return words.reshape(words.shape[0], 128, -1), scales


def unpack4(words, scales):
    return unpack_weight(words.reshape(words.shape[0], 128, -1, 2), scales, "e2m1")


B, S, H, HD = 8, 512, 512, 128
NH = H // HD
HALF = HD // 2
WS = 1.5 * (HD / H) ** 0.25 / np.sqrt(H)


def rotate_half(u):
    return np.concatenate((-u[..., HALF:], u[..., :HALF]), axis=-1)


def rope(u, c, s):
    u4 = u.reshape(B, S, NH, HD)
    return (u4 * c[None, :, None, :] + rotate_half(u4) * s[None, :, None, :]).reshape(B, S, H)


def draw0():
    s = mx_kscale(H)
    t = np.tile(mx_kscale(H).reshape(NH, 2, HALF)[:, :1, :], (1, 2, 1)).reshape(H)
    hidden_states = bf(np.random.standard_normal((B, S, H)) * s)
    wq_deq_words, wq_deq_scales = pack4((np.random.standard_normal((H, H)) * WS * t[:, None] / s[None, :]).T)
    wk_deq_words, wk_deq_scales = pack4((np.random.standard_normal((H, H)) * WS / t[:, None] / s[None, :]).T)
    return {"hidden_states": hidden_states,
            "wq_deq_words": wq_deq_words,
            "wq_deq_scales": wq_deq_scales,
            "wk_deq_words": wk_deq_words,
            "wk_deq_scales": wk_deq_scales,
            "cos": bf(np.random.random((S, HD))),
            "sin": bf(np.random.random((S, HD))),
            "attention_mask": bf(np.random.standard_normal((1, S, S)) * 0.5)}


def core(hidden_states, wq_deq_words, wq_deq_scales, wk_deq_words, wk_deq_scales, cos, sin, attention_mask):
    xq = mxq(f64(hidden_states), 2, "e4m3")
    q = xq @ unpack4(wq_deq_words, wq_deq_scales)
    k = xq @ unpack4(wk_deq_words, wk_deq_scales)
    q_rot = rope(q, f64(cos), f64(sin))
    k_rot = rope(k, f64(cos), f64(sin))
    scores = (mxq(q_rot, 2, "e4m3") @ mxq(k_rot, 2, "e4m3").transpose(0, 2, 1)) / np.sqrt(HD)
    return scores + f64(attention_mask)


def e4m3fn_bytes(y):
    return np.clip(np.asarray(y, np.float64), -448.0, 448.0).astype(np.float32).astype(ml_dtypes.float8_e4m3fn).view(np.uint8)


def e4m3fn_values(b):
    return np.asarray(b, np.uint8).view(ml_dtypes.float8_e4m3fn).astype(np.float64)


def setup_inputs():
    d = draw0()
    x0 = np.asarray(d['hidden_states']).astype(np.float64)
    s = (np.max(np.abs(x0), axis=(0, 1), keepdims=True) / 448.0).astype(np.float32)
    out = {}
    for k, v in d.items():
        if k == 'hidden_states':
            out['hidden_states_bytes'] = e4m3fn_bytes(x0 / s.astype(np.float64))
            out['hidden_states_scale'] = s
        else:
            out[k] = v
    return out


def reference(hidden_states_bytes, hidden_states_scale, wq_deq_words, wq_deq_scales, wk_deq_words, wk_deq_scales, cos, sin, attention_mask):
    return core(e4m3fn_values(hidden_states_bytes) * hidden_states_scale.astype(np.float64), wq_deq_words, wq_deq_scales, wk_deq_words, wk_deq_scales, cos, sin, attention_mask)

@@ -1,0 +1,385 @@
+from contextlib import ExitStack
+
+import concourse.mybir as mybir
+from concourse.masks import make_identity
+
+B, S, H, HD = 8, 512, 512, 128
+P = 128
+NT = B * S // P
+
+FLOPS = 2 * B * S * H * 2 * H + 2 * B * S * S * H
+
+F32 = mybir.dt.float32
+BF16 = mybir.dt.bfloat16
+I32 = mybir.dt.int32
+U32 = mybir.dt.uint32
+U8 = mybir.dt.uint8
+FP8 = mybir.dt.float8_e4m3fn
+FP8X4 = mybir.dt.float8_e4m3fn_x4
+FP4X4 = mybir.dt.float4_e2m1fn_x4
+MULT = mybir.AluOpType.mult
+ADD = mybir.AluOpType.add
+COPY = mybir.ActivationFunctionType.Copy
+INV = 1.0 / HD ** 0.5
+
+
+def tile_llamaattention_pa_t_w4_kernel(
+    tc, x_bytes, x_scale, wq_words, wq_scales, wk_words, wk_scales, cos, sin, mask, out
+):
+    nc = tc.nc
+    with ExitStack() as ctx:
+        keep = ctx.enter_context(tc.tile_pool(name="keep", bufs=1))
+        work = ctx.enter_context(tc.tile_pool(name="work", bufs=2))
+        prod = ctx.enter_context(tc.tile_pool(name="prod", bufs=3))
+        outp = ctx.enter_context(tc.tile_pool(name="outp", bufs=4))
+        ps_ab = ctx.enter_context(tc.psum_pool(name="ps_ab", bufs=3))
+        ps_t = ctx.enter_context(tc.psum_pool(name="ps_t", bufs=2))
+        ps_x = ctx.enter_context(tc.psum_pool(name="ps_x", bufs=1))
+        ps_s = ctx.enter_context(tc.psum_pool(name="ps_s", bufs=2))
+        ctx.enter_context(tc.manual_schedule())
+
+        ident = keep.tile([P, P], F32, name="ident")
+        make_identity(nc, ident[:])
+
+        xsc = keep.tile([P, 1, 2, 2], F32, name="xsc")
+        cosn = keep.tile([P, 4, HD], BF16, name="cosn")
+        sinn = keep.tile([P, 4, HD], BF16, name="sinn")
+        maskt = keep.tile([P, 4, S], BF16, name="maskt")
+        wraw = keep.tile([P, 2, 256], I32, name="wraw")
+        wsraw = keep.tile([P, 2, 128], I32, name="wsraw")
+        wp8 = keep.tile([P, 2, 1024], U8, name="wp8", align_bytes=64)
+        ws8 = keep.tile([P, 2, 512], U8, name="ws8", align_bytes=64)
+        tabc = keep.tile([P, 1, 4, 8, 64], BF16, name="tabc")
+        tabs = keep.tile([P, 1, 4, 8, 64], BF16, name="tabs")
+
+        nc.vector.memset(wsraw[:], 0)
+        xbs = []
+        for b in range(B):
+            xb = keep.tile([P, 4, H], U8, name="xb%d" % b)
+            xbs.append(xb)
+
+        def load_x(b):
+            nc.sync.dma_start(out=xbs[b][:], in_=x_bytes[b].rearrange("(tt p) k -> p tt k", p=P))
+
+        load_x(0)
+        nc.scalar.dma_start(
+            out=xsc[:].rearrange("p o u e -> p (o u e)"),
+            in_=x_scale.rearrange("a b (p t) -> p (a b t)", t=4),
+        )
+        nc.scalar.dma_start(out=cosn[:], in_=cos.rearrange("(st p) d -> p st d", p=P))
+        nc.scalar.dma_start(out=sinn[:], in_=sin.rearrange("(st p) d -> p st d", p=P))
+        nc.sync.dma_start(out=wraw[:, 0, :], in_=wq_words[0].bitcast(I32))
+        nc.sync.dma_start(out=wraw[:, 1, :], in_=wk_words[0].bitcast(I32))
+        for w, sc in ((0, wq_scales), (1, wk_scales)):
+            for q in range(4):
+                nc.sync.dma_start(
+                    out=wsraw[32 * q : 32 * q + 4, w, :], in_=sc[0, 4 * q : 4 * q + 4, :].bitcast(I32)
+                )
+        load_x(1)
+        nc.sync.dma_start(out=maskt[:], in_=mask[0].rearrange("(i p) j -> p i j", p=P))
+        for b in range(2, B):
+            load_x(b)
+
+        xw = {}
+        xt = {}
+        xp = {}
+        xi = {}
+        xc = {}
+        xs = {}
+        ab = {}
+        m1 = {}
+        m2 = {}
+        tp = {}
+        qi = {}
+        qc = {}
+        qs = {}
+        scp = {}
+
+        def widen(b, lo, hi):
+            if lo == 0:
+                t = work.tile([P, 4, H], BF16, name="xw")
+                xw[b] = t
+            nc.scalar.copy(out=xw[b][:, lo:hi, :], in_=xbs[b][:, lo:hi, :].bitcast(FP8))
+
+        def x_codes(b):
+            c = work.tile([P, S], U32, name="xc", align_bytes=64)
+            s = work.tile([P, S], U8, name="xs", align_bytes=64)
+            xc[b] = c
+            xs[b] = s
+
+        def x_quant(b, lo, hi):
+            nc.vector.quantize_mx(
+                out=xc[b][:, lo:hi].bitcast(FP8X4),
+                scales=xs[b][:, lo:hi],
+                in_=xi[b][:, lo:hi, :].rearrange("p n t -> p (n t)"),
+            )
+
+        def xtr_v(b, lo, hi, pool, tag):
+            t = pool.tile([P, 2, (hi - lo) * P], F32, name=tag)
+            xt[b, lo] = t
+            for tt in range(lo, hi):
+                words = xw[b][:, tt, :].bitcast(F32)
+                for u in range(2):
+                    nc.tensor.transpose(t[:, u, (tt - lo) * P : (tt - lo + 1) * P], words[:, u : 256 : 2], ident[:])
+
+        def xev_v(b, lo, hi):
+            if lo == 0:
+                xit = work.tile([P, S, 4], BF16, name="xi", align_bytes=64)
+                xi[b] = xit
+            t = xt.pop((b, lo))
+            nc.vector.tensor_tensor(
+                out=xi[b][:, lo * P : hi * P, :].rearrange("p n (u e) -> p n u e", u=2),
+                in0=t[:].bitcast(BF16).rearrange("p u (n e) -> p n u e", e=2),
+                in1=xsc[:].to_broadcast([P, (hi - lo) * P, 2, 2]),
+                op=MULT,
+            )
+
+        def xtr_half(b, u):
+            t = ps_x.tile([P, S], F32, name="xt")
+            xt[b, u] = t
+            for tt in range(4):
+                words = xw[b][:, tt, :].bitcast(F32)
+                nc.tensor.transpose(t[:, tt * P : tt * P + P], words[:, u : 256 : 2], ident[:])
+
+        def xev_half(b, u):
+            if u == 0:
+                pl = work.tile([P, 4, S], BF16, name="xp")
+                xp[b] = pl
+            view = xt.pop((b, u))[:].bitcast(BF16).rearrange("p (n e) -> p e n", e=2)
+            for e in range(2):
+                nc.scalar.activation(
+                    out=xp[b][:, 2 * u + e, :], in_=view[:, e, :], func=COPY, scale=xsc[:, 0, u, e : e + 1]
+                )
+
+        def interleave(b, hf):
+            if hf == 0:
+                xit = work.tile([P, S, 4], BF16, name="xi", align_bytes=64)
+                xi[b] = xit
+            cols = slice(hf * 256, hf * 256 + 256)
+            nc.gpsimd.tensor_scalar(
+                out=xi[b][:, cols, :],
+                in0=xp[b][:, :, cols].rearrange("p t n -> p n t"),
+                scalar1=1.0,
+                scalar2=0.0,
+                op0=MULT,
+                op1=ADD,
+            )
+
+        def proj(n):
+            b, tt = divmod(n, 4)
+            cols = slice(tt * P, tt * P + P)
+            for h in range(2):
+                a = ps_ab.tile([P, 2, 4, 64], F32, name="ab")
+                ab[n, h] = a
+                nc.tensor.matmul_mx(
+                    out=a[:].rearrange("p k t m -> p (k t m)"),
+                    lhsT=xc[b][:, cols].bitcast(FP8X4),
+                    lhsT_scale=xs[b][:, cols],
+                    rhs=wp8[:, h, :].bitcast(FP4X4),
+                    rhs_scale=ws8[:, h, :],
+                    start=True,
+                    stop=True,
+                )
+
+        def product(n, h):
+            st = n % 4
+            if h == 0:
+                a1 = prod.tile([P, 2, 4, 2, 64], F32, name="m1")
+                a2 = prod.tile([P, 2, 4, 2, 64], F32, name="m2")
+                m1[n] = a1
+                m2[n] = a2
+            a = ab.pop((n, h))
+            nc.vector.tensor_tensor(
+                out=m1[n][:, :, :, h, :],
+                in0=a[:],
+                in1=tabc[:, :, :, 2 * st + h, :].to_broadcast([P, 2, 4, 64]),
+                op=MULT,
+            )
+            nc.vector.tensor_tensor(
+                out=m2[n][:, :, :, 1 - h, :],
+                in0=a[:],
+                in1=tabs[:, :, :, 2 * st + 1 - h, :].to_broadcast([P, 2, 4, 64]),
+                op=MULT,
+            )
+
+        def turn(n):
+            for w in range(2):
+                t4 = ps_t.tile([P, 4, P], F32, name="tp")
+                tp[n, w] = t4
+                for t in range(4):
+                    for m, first in ((m1[n], True), (m2[n], False)):
+                        nc.tensor.matmul(
+                            t4[:, t, :],
+                            lhsT=m[:, w, t, :, :].rearrange("p h m -> p (h m)"),
+                            rhs=ident[:],
+                            start=first,
+                            stop=not first,
+                            is_transpose=True,
+                        )
+
+        def turn_out(n):
+            b, tt = divmod(n, 4)
+            for w in range(2):
+                if tt == 0:
+                    ti = work.tile([P, S, 4], BF16, name="qi%d" % w, align_bytes=64)
+                    c = work.tile([P, S], U32, name="qc%d" % w, align_bytes=64)
+                    s = work.tile([P, S], U8, name="qs%d" % w, align_bytes=64)
+                    qi[b, w] = ti
+                    qc[b, w] = c
+                    qs[b, w] = s
+                dst = qi[b, w][:, tt * P : tt * P + P, :]
+                view = tp.pop((n, w))[:].rearrange("p t n -> p n t")
+                if n == NT - 1 and w == 1:
+                    nc.vector.tensor_copy(out=dst, in_=view)
+                else:
+                    nc.scalar.copy(out=dst, in_=view)
+
+        def quant(b, w, lo=0, hi=S):
+            nc.vector.quantize_mx(
+                out=qc[b, w][:, lo:hi].bitcast(FP8X4),
+                scales=qs[b, w][:, lo:hi],
+                in_=qi[b, w][:, lo:hi, :].rearrange("p n t -> p (n t)"),
+            )
+
+        def score(b, i):
+            cols = slice(i * P, i * P + P)
+            t = ps_s.tile([P, S], F32, name="sc")
+            scp[b, i] = t
+            nc.tensor.matmul_mx(
+                out=t[:],
+                lhsT=qc[b, 0][:, cols].bitcast(FP8X4),
+                lhsT_scale=qs[b, 0][:, cols],
+                rhs=qc[b, 1][:].bitcast(FP8X4),
+                rhs_scale=qs[b, 1][:],
+                start=True,
+                stop=True,
+            )
+
+        def finish(b, i):
+            t = scp.pop((b, i))
+            o = outp.tile([P, S], F32, name="o")
+            if b == B - 1 and i != 1:
+                nc.vector.scalar_tensor_tensor(
+                    out=o[:], in0=t[:], scalar=INV, in1=maskt[:, i, :], op0=MULT, op1=ADD
+                )
+            else:
+                sc1 = outp.tile([P, S], F32, name="sc1")
+                nc.scalar.activation(out=sc1[:], in_=t[:], func=COPY, scale=INV)
+                nc.gpsimd.tensor_tensor(out=o[:], in0=sc1[:], in1=maskt[:, i, :], op=ADD)
+            nc.sync.dma_start(out=out[b, i * P : i * P + P, :], in_=o[:])
+
+        def permute(raw, dst, engine):
+            for h in range(2):
+                d = dst[:, h, :].bitcast(I32).rearrange("p (w t g c e) -> p w t g c e", w=2, t=4, g=2, c=4)
+                for w in range(2):
+                    s = raw[:, w, :].rearrange("p (c h g t e) -> p c h g t e", c=4, h=2, g=2, t=4)
+                    for g in range(2):
+                        engine.tensor_copy(
+                            out=d[:, w, :, g, :, :], in_=s[:, :, h, g, :, :].rearrange("p c t e -> p t c e")
+                        )
+
+        def table(src, dst, engine_copy, lo, hi):
+            view = src[:, lo:hi, :].rearrange("p st d -> p (st d)").rearrange("p (a t o e) -> p a t o e", t=4, o=1, e=8)
+            a = 4 * (hi - lo)
+            for t in range(4):
+                engine_copy(
+                    out=dst[:, 0, t, 2 * lo : 2 * hi, :].rearrange("p s m -> p (s m)").rearrange(
+                        "p (a c e) -> p a c e", c=4, e=8
+                    ),
+                    in_=view[:, :, t, :, :].to_broadcast([P, a, 4, 8]),
+                )
+
+        for tt in range(4):
+            widen(0, tt, tt + 1)
+        nc.vector.tensor_scalar(out=sinn[:, :, 0:64], in0=sinn[:, :, 0:64], scalar1=-1.0, scalar2=None, op0=MULT)
+        table(cosn, tabc, nc.vector.tensor_copy, 0, 1)
+        table(sinn, tabs, nc.vector.tensor_copy, 0, 1)
+        permute(wsraw, ws8, nc.gpsimd)
+        x_codes(0)
+        xtr_v(0, 0, 1, ps_x, "xt")
+        xtr_v(0, 1, 2, ps_s, "sc")
+        xtr_v(0, 2, 3, ps_s, "sc")
+        xev_v(0, 0, 1)
+        x_quant(0, 0, P)
+        xtr_v(0, 3, 4, ps_x, "xt")
+        permute(wraw, wp8, nc.vector)
+        table(cosn, tabc, nc.scalar.copy, 1, 4)
+        table(sinn, tabs, nc.scalar.copy, 1, 4)
+        proj(0)
+        for tt in range(1, 4):
+            xev_v(0, tt, tt + 1)
+            x_quant(0, tt * P, tt * P + P)
+        widen(1, 0, 4)
+        widen(2, 0, 4)
+
+        for n in range(NT + 1):
+            b, k = divmod(n, 4)
+            if k == 2 and b > 0:
+                finish(b - 1, 0)
+            if k == 3 and b > 0:
+                finish(b - 1, 1)
+            if k == 0 and b > 1:
+                finish(b - 2, 2)
+                finish(b - 2, 3)
+            if 0 <= n - 1 < NT:
+                turn(n - 1)
+            if n < NT:
+                product(n, 0)
+            if 0 <= n - 1 < NT:
+                turn_out(n - 1)
+            if k == 1 and b + 3 < B:
+                widen(b + 3, 0, 2)
+            if k == 3 and b + 3 < B:
+                widen(b + 3, 2, 4)
+            if k == 1 and b + 2 < B:
+                xev_half(b + 2, 0)
+            if k == 2 and b + 2 < B:
+                xev_half(b + 2, 1)
+                interleave(b + 2, 0)
+            if k == 3 and b + 2 < B:
+                interleave(b + 2, 1)
+            if n == 1:
+                xev_v(1, 0, 2)
+                xev_v(1, 2, 4)
+            if n == 2:
+                x_codes(1)
+                x_quant(1, 0, S)
+            if k == 1 and 0 < b < B:
+                quant(b - 1, 0)
+                quant(b - 1, 1)
+                if b + 1 < B:
+                    x_codes(b + 1)
+                    x_quant(b + 1, 0, S)
+            if n == NT - 1:
+                quant(B - 1, 0, 0, 256)
+                quant(B - 1, 1, 0, 256)
+            if n == NT:
+                for w in range(2):
+                    quant(B - 1, w, 256, 384)
+                for w in range(2):
+                    quant(B - 1, w, 384, S)
+            if k == 0 and b + 2 < B:
+                xtr_half(b + 2, 0)
+            if k == 1 and b + 2 < B:
+                xtr_half(b + 2, 1)
+            if n + 1 < NT:
+                proj(n + 1)
+            if n == 0:
+                xtr_v(1, 0, 2, ps_s, "sc")
+                xtr_v(1, 2, 4, ps_s, "sc")
+            if k == 1 and 0 < b < B:
+                score(b - 1, 0)
+            if k == 2 and 0 < b < B:
+                score(b - 1, 1)
+            if k == 3 and 0 < b < B:
+                score(b - 1, 2)
+                score(b - 1, 3)
+            if n < NT:
+                product(n, 1)
+            if n == NT:
+                for i in range(2):
+                    score(B - 1, i)
+                for i in range(4):
+                    finish(B - 1, i)
+                    if i < 2:
+                        score(B - 1, i + 2)

@@ -32,14 +32,12 @@ def tile_llamaattention_pa_t_w4_kernel(
         work = ctx.enter_context(tc.tile_pool(name="work", bufs=2))
         prod = ctx.enter_context(tc.tile_pool(name="prod", bufs=3))
         outp = ctx.enter_context(tc.tile_pool(name="outp", bufs=4))
-        ps_ab = ctx.enter_context(tc.psum_pool(name="ps_ab", bufs=3))
+        ps_ab = ctx.enter_context(tc.psum_pool(name="ps_ab", bufs=4))
         ps_t = ctx.enter_context(tc.psum_pool(name="ps_t", bufs=2))
-        ps_x = ctx.enter_context(tc.psum_pool(name="ps_x", bufs=1))
         ps_s = ctx.enter_context(tc.psum_pool(name="ps_s", bufs=2))
         ctx.enter_context(tc.manual_schedule())
 
         ident = keep.tile([P, P], F32, name="ident")
-        make_identity(nc, ident[:])
 
         xsc = keep.tile([P, 1, 2, 2], F32, name="xsc")
         cosn = keep.tile([P, 4, HD], BF16, name="cosn")
@@ -66,8 +64,9 @@ def tile_llamaattention_pa_t_w4_kernel(
             out=xsc[:].rearrange("p o u e -> p (o u e)"),
             in_=x_scale.rearrange("a b (p t) -> p (a b t)", t=4),
         )
-        nc.scalar.dma_start(out=cosn[:], in_=cos.rearrange("(st p) d -> p st d", p=P))
-        nc.scalar.dma_start(out=sinn[:], in_=sin.rearrange("(st p) d -> p st d", p=P))
+        nc.gpsimd.dma_start(out=cosn[:], in_=cos.rearrange("(st p) d -> p st d", p=P))
+        nc.gpsimd.dma_start(out=sinn[:], in_=sin.rearrange("(st p) d -> p st d", p=P))
+        make_identity(nc, ident[:])
         nc.sync.dma_start(out=wraw[:, 0, :], in_=wq_words[0].bitcast(I32))
         nc.sync.dma_start(out=wraw[:, 1, :], in_=wk_words[0].bitcast(I32))
         for w, sc in ((0, wq_scales), (1, wk_scales)):
@@ -135,7 +134,7 @@ def tile_llamaattention_pa_t_w4_kernel(
             )
 
         def xtr_half(b, u):
-            t = ps_x.tile([P, S], F32, name="xt")
+            t = ps_s.tile([P, S], F32, name="sc")
             xt[b, u] = t
             for tt in range(4):
                 words = xw[b][:, tt, :].bitcast(F32)
@@ -291,25 +290,32 @@ def tile_llamaattention_pa_t_w4_kernel(
 
         for tt in range(4):
             widen(0, tt, tt + 1)
+        widen(1, 0, 4)
+        permute(wraw, wp8, nc.vector)
+        x_codes(0)
+        xtr_v(0, 0, 1, ps_s, "sc")
+        xtr_v(0, 1, 2, ps_s, "sc")
+        xev_v(0, 0, 1)
+        x_quant(0, 0, P)
+        xtr_v(0, 2, 3, ps_s, "sc")
         nc.vector.tensor_scalar(out=sinn[:, :, 0:64], in0=sinn[:, :, 0:64], scalar1=-1.0, scalar2=None, op0=MULT)
         table(cosn, tabc, nc.vector.tensor_copy, 0, 1)
         table(sinn, tabs, nc.vector.tensor_copy, 0, 1)
-        permute(wsraw, ws8, nc.gpsimd)
-        x_codes(0)
-        xtr_v(0, 0, 1, ps_x, "xt")
-        xtr_v(0, 1, 2, ps_s, "sc")
-        xtr_v(0, 2, 3, ps_s, "sc")
-        xev_v(0, 0, 1)
-        x_quant(0, 0, P)
-        xtr_v(0, 3, 4, ps_x, "xt")
-        permute(wraw, wp8, nc.vector)
+        permute(wsraw, ws8, nc.vector)
         table(cosn, tabc, nc.scalar.copy, 1, 4)
         table(sinn, tabs, nc.scalar.copy, 1, 4)
         proj(0)
         for tt in range(1, 4):
             xev_v(0, tt, tt + 1)
             x_quant(0, tt * P, tt * P + P)
-        widen(1, 0, 4)
+            if tt == 1:
+                xtr_v(0, 3, 4, ps_s, "sc")
+        xtr_half(1, 0)
+        xtr_half(1, 1)
+        xev_half(1, 0)
+        xev_half(1, 1)
+        interleave(1, 0)
+        interleave(1, 1)
         widen(2, 0, 4)
 
         for n in range(NT + 1):
@@ -318,29 +324,34 @@ def tile_llamaattention_pa_t_w4_kernel(
                 finish(b - 1, 0)
             if k == 3 and b > 0:
                 finish(b - 1, 1)
+                finish(b - 1, 2)
             if k == 0 and b > 1:
-                finish(b - 2, 2)
                 finish(b - 2, 3)
+            if k == 1 and b + 2 < B:
+                xev_half(b + 2, 0)
+            if k == 2 and b + 2 < B:
+                xev_half(b + 2, 1)
+            if n + 1 < NT:
+                proj(n + 1)
             if 0 <= n - 1 < NT:
                 turn(n - 1)
             if n < NT:
                 product(n, 0)
+            if n == NT:
+                for w in range(2):
+                    quant(B - 1, w, 0, 256)
+                for w in range(2):
+                    quant(B - 1, w, 256, 384)
             if 0 <= n - 1 < NT:
                 turn_out(n - 1)
             if k == 1 and b + 3 < B:
                 widen(b + 3, 0, 2)
             if k == 3 and b + 3 < B:
                 widen(b + 3, 2, 4)
-            if k == 1 and b + 2 < B:
-                xev_half(b + 2, 0)
             if k == 2 and b + 2 < B:
-                xev_half(b + 2, 1)
                 interleave(b + 2, 0)
             if k == 3 and b + 2 < B:
                 interleave(b + 2, 1)
-            if n == 1:
-                xev_v(1, 0, 2)
-                xev_v(1, 2, 4)
             if n == 2:
                 x_codes(1)
                 x_quant(1, 0, S)
@@ -350,29 +361,19 @@ def tile_llamaattention_pa_t_w4_kernel(
                 if b + 1 < B:
                     x_codes(b + 1)
                     x_quant(b + 1, 0, S)
-            if n == NT - 1:
-                quant(B - 1, 0, 0, 256)
-                quant(B - 1, 1, 0, 256)
             if n == NT:
-                for w in range(2):
-                    quant(B - 1, w, 256, 384)
                 for w in range(2):
                     quant(B - 1, w, 384, S)
             if k == 0 and b + 2 < B:
                 xtr_half(b + 2, 0)
             if k == 1 and b + 2 < B:
                 xtr_half(b + 2, 1)
-            if n + 1 < NT:
-                proj(n + 1)
-            if n == 0:
-                xtr_v(1, 0, 2, ps_s, "sc")
-                xtr_v(1, 2, 4, ps_s, "sc")
             if k == 1 and 0 < b < B:
                 score(b - 1, 0)
             if k == 2 and 0 < b < B:
                 score(b - 1, 1)
-            if k == 3 and 0 < b < B:
                 score(b - 1, 2)
+            if k == 3 and 0 < b < B:
                 score(b - 1, 3)
             if n < NT:
                 product(n, 1)

from contextlib import ExitStack

import concourse.mybir as mybir
from concourse.masks import make_identity

B, S, H, HD = 8, 512, 512, 128
P = 128
NT = B * S // P

FLOPS = 2 * B * S * H * 2 * H + 2 * B * S * S * H

F32 = mybir.dt.float32
BF16 = mybir.dt.bfloat16
I32 = mybir.dt.int32
U32 = mybir.dt.uint32
U8 = mybir.dt.uint8
FP8 = mybir.dt.float8_e4m3fn
FP8X4 = mybir.dt.float8_e4m3fn_x4
FP4X4 = mybir.dt.float4_e2m1fn_x4
MULT = mybir.AluOpType.mult
ADD = mybir.AluOpType.add
COPY = mybir.ActivationFunctionType.Copy
INV = 1.0 / HD ** 0.5


def tile_llamaattention_pa_t_w4_kernel(
    tc, x_bytes, x_scale, wq_words, wq_scales, wk_words, wk_scales, cos, sin, mask, out
):
    nc = tc.nc
    with ExitStack() as ctx:
        keep = ctx.enter_context(tc.tile_pool(name="keep", bufs=1))
        work = ctx.enter_context(tc.tile_pool(name="work", bufs=2))
        prod = ctx.enter_context(tc.tile_pool(name="prod", bufs=3))
        outp = ctx.enter_context(tc.tile_pool(name="outp", bufs=4))
        ps_ab = ctx.enter_context(tc.psum_pool(name="ps_ab", bufs=4))
        ps_t = ctx.enter_context(tc.psum_pool(name="ps_t", bufs=2))
        ps_s = ctx.enter_context(tc.psum_pool(name="ps_s", bufs=2))
        ctx.enter_context(tc.manual_schedule())

        ident = keep.tile([P, P], F32, name="ident")

        xsc = keep.tile([P, 1, 2, 2], F32, name="xsc")
        cosn = keep.tile([P, 4, HD], BF16, name="cosn")
        sinn = keep.tile([P, 4, HD], BF16, name="sinn")
        maskt = keep.tile([P, 4, S], BF16, name="maskt")
        wraw = keep.tile([P, 2, 256], I32, name="wraw")
        wsraw = keep.tile([P, 2, 128], I32, name="wsraw")
        wp8 = keep.tile([P, 2, 1024], U8, name="wp8", align_bytes=64)
        ws8 = keep.tile([P, 2, 512], U8, name="ws8", align_bytes=64)
        tabc = keep.tile([P, 1, 4, 8, 64], BF16, name="tabc")
        tabs = keep.tile([P, 1, 4, 8, 64], BF16, name="tabs")

        nc.vector.memset(wsraw[:], 0)
        xbs = []
        for b in range(B):
            xb = keep.tile([P, 4, H], U8, name="xb%d" % b)
            xbs.append(xb)

        def load_x(b):
            nc.sync.dma_start(out=xbs[b][:], in_=x_bytes[b].rearrange("(tt p) k -> p tt k", p=P))

        load_x(0)
        nc.scalar.dma_start(
            out=xsc[:].rearrange("p o u e -> p (o u e)"),
            in_=x_scale.rearrange("a b (p t) -> p (a b t)", t=4),
        )
        nc.gpsimd.dma_start(out=cosn[:], in_=cos.rearrange("(st p) d -> p st d", p=P))
        nc.gpsimd.dma_start(out=sinn[:], in_=sin.rearrange("(st p) d -> p st d", p=P))
        make_identity(nc, ident[:])
        nc.sync.dma_start(out=wraw[:, 0, :], in_=wq_words[0].bitcast(I32))
        nc.sync.dma_start(out=wraw[:, 1, :], in_=wk_words[0].bitcast(I32))
        for w, sc in ((0, wq_scales), (1, wk_scales)):
            for q in range(4):
                nc.sync.dma_start(
                    out=wsraw[32 * q : 32 * q + 4, w, :], in_=sc[0, 4 * q : 4 * q + 4, :].bitcast(I32)
                )
        load_x(1)
        nc.sync.dma_start(out=maskt[:], in_=mask[0].rearrange("(i p) j -> p i j", p=P))
        for b in range(2, B):
            load_x(b)

        xw = {}
        xt = {}
        xp = {}
        xi = {}
        xc = {}
        xs = {}
        ab = {}
        m1 = {}
        m2 = {}
        tp = {}
        qi = {}
        qc = {}
        qs = {}
        scp = {}

        def widen(b, lo, hi):
            if lo == 0:
                t = work.tile([P, 4, H], BF16, name="xw")
                xw[b] = t
            nc.scalar.copy(out=xw[b][:, lo:hi, :], in_=xbs[b][:, lo:hi, :].bitcast(FP8))

        def x_codes(b):
            c = work.tile([P, S], U32, name="xc", align_bytes=64)
            s = work.tile([P, S], U8, name="xs", align_bytes=64)
            xc[b] = c
            xs[b] = s

        def x_quant(b, lo, hi):
            nc.vector.quantize_mx(
                out=xc[b][:, lo:hi].bitcast(FP8X4),
                scales=xs[b][:, lo:hi],
                in_=xi[b][:, lo:hi, :].rearrange("p n t -> p (n t)"),
            )

        def xtr_v(b, lo, hi, pool, tag):
            t = pool.tile([P, 2, (hi - lo) * P], F32, name=tag)
            xt[b, lo] = t
            for tt in range(lo, hi):
                words = xw[b][:, tt, :].bitcast(F32)
                for u in range(2):
                    nc.tensor.transpose(t[:, u, (tt - lo) * P : (tt - lo + 1) * P], words[:, u : 256 : 2], ident[:])

        def xev_v(b, lo, hi):
            if lo == 0:
                xit = work.tile([P, S, 4], BF16, name="xi", align_bytes=64)
                xi[b] = xit
            t = xt.pop((b, lo))
            nc.vector.tensor_tensor(
                out=xi[b][:, lo * P : hi * P, :].rearrange("p n (u e) -> p n u e", u=2),
                in0=t[:].bitcast(BF16).rearrange("p u (n e) -> p n u e", e=2),
                in1=xsc[:].to_broadcast([P, (hi - lo) * P, 2, 2]),
                op=MULT,
            )

        def xtr_half(b, u):
            t = ps_s.tile([P, S], F32, name="sc")
            xt[b, u] = t
            for tt in range(4):
                words = xw[b][:, tt, :].bitcast(F32)
                nc.tensor.transpose(t[:, tt * P : tt * P + P], words[:, u : 256 : 2], ident[:])

        def xev_half(b, u):
            if u == 0:
                pl = work.tile([P, 4, S], BF16, name="xp")
                xp[b] = pl
            view = xt.pop((b, u))[:].bitcast(BF16).rearrange("p (n e) -> p e n", e=2)
            for e in range(2):
                nc.scalar.activation(
                    out=xp[b][:, 2 * u + e, :], in_=view[:, e, :], func=COPY, scale=xsc[:, 0, u, e : e + 1]
                )

        def interleave(b, hf):
            if hf == 0:
                xit = work.tile([P, S, 4], BF16, name="xi", align_bytes=64)
                xi[b] = xit
            cols = slice(hf * 256, hf * 256 + 256)
            nc.gpsimd.tensor_scalar(
                out=xi[b][:, cols, :],
                in0=xp[b][:, :, cols].rearrange("p t n -> p n t"),
                scalar1=1.0,
                scalar2=0.0,
                op0=MULT,
                op1=ADD,
            )

        def proj(n):
            b, tt = divmod(n, 4)
            cols = slice(tt * P, tt * P + P)
            for h in range(2):
                a = ps_ab.tile([P, 2, 4, 64], F32, name="ab")
                ab[n, h] = a
                nc.tensor.matmul_mx(
                    out=a[:].rearrange("p k t m -> p (k t m)"),
                    lhsT=xc[b][:, cols].bitcast(FP8X4),
                    lhsT_scale=xs[b][:, cols],
                    rhs=wp8[:, h, :].bitcast(FP4X4),
                    rhs_scale=ws8[:, h, :],
                    start=True,
                    stop=True,
                )

        def product(n, h):
            st = n % 4
            if h == 0:
                a1 = prod.tile([P, 2, 4, 2, 64], F32, name="m1")
                a2 = prod.tile([P, 2, 4, 2, 64], F32, name="m2")
                m1[n] = a1
                m2[n] = a2
            a = ab.pop((n, h))
            nc.vector.tensor_tensor(
                out=m1[n][:, :, :, h, :],
                in0=a[:],
                in1=tabc[:, :, :, 2 * st + h, :].to_broadcast([P, 2, 4, 64]),
                op=MULT,
            )
            nc.vector.tensor_tensor(
                out=m2[n][:, :, :, 1 - h, :],
                in0=a[:],
                in1=tabs[:, :, :, 2 * st + 1 - h, :].to_broadcast([P, 2, 4, 64]),
                op=MULT,
            )

        def turn(n):
            for w in range(2):
                t4 = ps_t.tile([P, 4, P], F32, name="tp")
                tp[n, w] = t4
                for t in range(4):
                    for m, first in ((m1[n], True), (m2[n], False)):
                        nc.tensor.matmul(
                            t4[:, t, :],
                            lhsT=m[:, w, t, :, :].rearrange("p h m -> p (h m)"),
                            rhs=ident[:],
                            start=first,
                            stop=not first,
                            is_transpose=True,
                        )

        def turn_out(n):
            b, tt = divmod(n, 4)
            for w in range(2):
                if tt == 0:
                    ti = work.tile([P, S, 4], BF16, name="qi%d" % w, align_bytes=64)
                    c = work.tile([P, S], U32, name="qc%d" % w, align_bytes=64)
                    s = work.tile([P, S], U8, name="qs%d" % w, align_bytes=64)
                    qi[b, w] = ti
                    qc[b, w] = c
                    qs[b, w] = s
                dst = qi[b, w][:, tt * P : tt * P + P, :]
                view = tp.pop((n, w))[:].rearrange("p t n -> p n t")
                if n == NT - 1 and w == 1:
                    nc.vector.tensor_copy(out=dst, in_=view)
                else:
                    nc.scalar.copy(out=dst, in_=view)

        def quant(b, w, lo=0, hi=S):
            nc.vector.quantize_mx(
                out=qc[b, w][:, lo:hi].bitcast(FP8X4),
                scales=qs[b, w][:, lo:hi],
                in_=qi[b, w][:, lo:hi, :].rearrange("p n t -> p (n t)"),
            )

        def score(b, i):
            cols = slice(i * P, i * P + P)
            t = ps_s.tile([P, S], F32, name="sc")
            scp[b, i] = t
            nc.tensor.matmul_mx(
                out=t[:],
                lhsT=qc[b, 0][:, cols].bitcast(FP8X4),
                lhsT_scale=qs[b, 0][:, cols],
                rhs=qc[b, 1][:].bitcast(FP8X4),
                rhs_scale=qs[b, 1][:],
                start=True,
                stop=True,
            )

        def finish(b, i):
            t = scp.pop((b, i))
            o = outp.tile([P, S], F32, name="o")
            if b == B - 1 and i != 1:
                nc.vector.scalar_tensor_tensor(
                    out=o[:], in0=t[:], scalar=INV, in1=maskt[:, i, :], op0=MULT, op1=ADD
                )
            else:
                sc1 = outp.tile([P, S], F32, name="sc1")
                nc.scalar.activation(out=sc1[:], in_=t[:], func=COPY, scale=INV)
                nc.gpsimd.tensor_tensor(out=o[:], in0=sc1[:], in1=maskt[:, i, :], op=ADD)
            nc.sync.dma_start(out=out[b, i * P : i * P + P, :], in_=o[:])

        def permute(raw, dst, engine):
            for h in range(2):
                d = dst[:, h, :].bitcast(I32).rearrange("p (w t g c e) -> p w t g c e", w=2, t=4, g=2, c=4)
                for w in range(2):
                    s = raw[:, w, :].rearrange("p (c h g t e) -> p c h g t e", c=4, h=2, g=2, t=4)
                    for g in range(2):
                        engine.tensor_copy(
                            out=d[:, w, :, g, :, :], in_=s[:, :, h, g, :, :].rearrange("p c t e -> p t c e")
                        )

        def table(src, dst, engine_copy, lo, hi):
            view = src[:, lo:hi, :].rearrange("p st d -> p (st d)").rearrange("p (a t o e) -> p a t o e", t=4, o=1, e=8)
            a = 4 * (hi - lo)
            for t in range(4):
                engine_copy(
                    out=dst[:, 0, t, 2 * lo : 2 * hi, :].rearrange("p s m -> p (s m)").rearrange(
                        "p (a c e) -> p a c e", c=4, e=8
                    ),
                    in_=view[:, :, t, :, :].to_broadcast([P, a, 4, 8]),
                )

        for tt in range(4):
            widen(0, tt, tt + 1)
        widen(1, 0, 4)
        permute(wraw, wp8, nc.vector)
        x_codes(0)
        xtr_v(0, 0, 1, ps_s, "sc")
        xtr_v(0, 1, 2, ps_s, "sc")
        xev_v(0, 0, 1)
        x_quant(0, 0, P)
        xtr_v(0, 2, 3, ps_s, "sc")
        nc.vector.tensor_scalar(out=sinn[:, :, 0:64], in0=sinn[:, :, 0:64], scalar1=-1.0, scalar2=None, op0=MULT)
        table(cosn, tabc, nc.vector.tensor_copy, 0, 1)
        table(sinn, tabs, nc.vector.tensor_copy, 0, 1)
        permute(wsraw, ws8, nc.vector)
        table(cosn, tabc, nc.scalar.copy, 1, 4)
        table(sinn, tabs, nc.scalar.copy, 1, 4)
        proj(0)
        for tt in range(1, 4):
            xev_v(0, tt, tt + 1)
            x_quant(0, tt * P, tt * P + P)
            if tt == 1:
                xtr_v(0, 3, 4, ps_s, "sc")
        xtr_half(1, 0)
        xtr_half(1, 1)
        xev_half(1, 0)
        xev_half(1, 1)
        interleave(1, 0)
        interleave(1, 1)
        widen(2, 0, 4)

        for n in range(NT + 1):
            b, k = divmod(n, 4)
            if k == 2 and b > 0:
                finish(b - 1, 0)
            if k == 3 and b > 0:
                finish(b - 1, 1)
                finish(b - 1, 2)
            if k == 0 and b > 1:
                finish(b - 2, 3)
            if k == 1 and b + 2 < B:
                xev_half(b + 2, 0)
            if k == 2 and b + 2 < B:
                xev_half(b + 2, 1)
            if n + 1 < NT:
                proj(n + 1)
            if 0 <= n - 1 < NT:
                turn(n - 1)
            if n < NT:
                product(n, 0)
            if n == NT:
                for w in range(2):
                    quant(B - 1, w, 0, 256)
                for w in range(2):
                    quant(B - 1, w, 256, 384)
            if 0 <= n - 1 < NT:
                turn_out(n - 1)
            if k == 1 and b + 3 < B:
                widen(b + 3, 0, 2)
            if k == 3 and b + 3 < B:
                widen(b + 3, 2, 4)
            if k == 2 and b + 2 < B:
                interleave(b + 2, 0)
            if k == 3 and b + 2 < B:
                interleave(b + 2, 1)
            if n == 2:
                x_codes(1)
                x_quant(1, 0, S)
            if k == 1 and 0 < b < B:
                quant(b - 1, 0)
                quant(b - 1, 1)
                if b + 1 < B:
                    x_codes(b + 1)
                    x_quant(b + 1, 0, S)
            if n == NT:
                for w in range(2):
                    quant(B - 1, w, 384, S)
            if k == 0 and b + 2 < B:
                xtr_half(b + 2, 0)
            if k == 1 and b + 2 < B:
                xtr_half(b + 2, 1)
            if k == 1 and 0 < b < B:
                score(b - 1, 0)
            if k == 2 and 0 < b < B:
                score(b - 1, 1)
                score(b - 1, 2)
            if k == 3 and 0 < b < B:
                score(b - 1, 3)
            if n < NT:
                product(n, 1)
            if n == NT:
                for i in range(2):
                    score(B - 1, i)
                for i in range(4):
                    finish(B - 1, i)
                    if i < 2:
                        score(B - 1, i + 2)
